import numpy as np
import ml_dtypes


def mxq(x, axis, fmt="e4m3"):
    dtype, down = {"e4m3": (ml_dtypes.float8_e4m3fn, 7), "e5m2": (ml_dtypes.float8_e5m2, 14)}[fmt]
    v = np.moveaxis(np.asarray(x, np.float32).astype(ml_dtypes.bfloat16).astype(np.float64), axis, -1)
    blocks = v.reshape(v.shape[:-1] + (-1, 32))
    amax = np.abs(blocks).max(-1, keepdims=True)
    byte = np.maximum(np.where(amax > 0, np.frexp(amax)[1] - 1 + 127, 0) - down, 1)
    scale = np.exp2(byte - 127.0)
    codes = (blocks / scale).astype(np.float32).astype(dtype).astype(np.float64)
    return np.moveaxis((codes * scale).reshape(v.shape), -1, axis)


WIDE = False


def mx_kscale(k):
    if not WIDE:
        return np.ones(k)
    levels = np.array([10, -10, 5, -5, 0])
    a = np.random.permutation(np.resize(levels, k // 512 * 4)).reshape(k // 512, 4)
    idx = np.arange(k)
    return np.exp2(a[idx // 512, idx % 128 // 32])


BF16 = ml_dtypes.bfloat16


def bf(x):
    return np.asarray(x, np.float32).astype(BF16)


def f64(x):
    return np.asarray(x).astype(np.float64)


B, S, D, E, NS, C = 1, 128, 1024, 512, 256, 512


def softmax(z):
    e = np.exp(z - z.max(-1, keepdims=True))
    return e / e.sum(-1, keepdims=True)


def setup_inputs():
    s, t = mx_kscale(D), mx_kscale(E)
    return {"x": bf(np.random.standard_normal((B, S, D)) * s),
            "Wk": bf(np.random.standard_normal((D, E)) / np.sqrt(D) / s[:, None] * t),
            "bk": bf(np.random.standard_normal(E) * 0.2 * t),
            "Wq": bf(np.random.standard_normal((D, E)) / np.sqrt(D) / s[:, None] * t),
            "bq": bf(np.random.standard_normal(E) * 0.2 * t),
            "slot_keys": bf(np.random.standard_normal((NS, E)) / t),
            "scale": bf((2.0 + 0.2 * np.random.standard_normal(1)) / np.sqrt(E))}


def reference(x, Wk, bk, Wq, bq, slot_keys, scale):
    xq = mxq(f64(x), 2, "e4m3")
    sq = mxq(f64(slot_keys), 1, "e4m3")
    k = (xq @ mxq(f64(Wk), 0, "e4m3")) + f64(bk)
    q = (xq @ mxq(f64(Wq), 0, "e4m3")) + f64(bq)
    ww = softmax((mxq(k, 2, "e4m3") @ sq.T) * f64(scale))
    rw = softmax((mxq(q, 2, "e4m3") @ sq.T) * f64(scale))
    return ww, rw

@@ -1,0 +1,202 @@
+from contextlib import ExitStack
+
+import concourse.mybir as mybir
+from concourse.masks import make_identity
+
+BF16 = mybir.dt.bfloat16
+F32 = mybir.dt.float32
+U32 = mybir.dt.uint32
+U8 = mybir.dt.uint8
+FP8X4 = mybir.dt.float8_e4m3fn_x4
+ALU = mybir.AluOpType
+ACT = mybir.ActivationFunctionType
+
+P = 128
+PACK = 4
+K_PASS = P * PACK
+HALVES = 2
+
+S, D, E, NS = 128, 1024, 512, 256
+D_PASSES = D // K_PASS
+E_TILES = E // P
+SLOT_TILES = NS // P
+
+FLOPS = 2 * (2 * S * D * E) + 2 * (2 * S * E * NS)
+
+
+def transpose_every_second_word(nc, bank_cols, rows_bf16, ident):
+    words = rows_bf16.bitcast(F32).rearrange("r (p u) -> r u p", u=HALVES)
+    for u in range(HALVES):
+        nc.tensor.transpose(bank_cols[:, u, :], words[:, u, :], ident)
+
+
+def tile_slotmemoryphasor_pa_s_kernel(
+    tc, x, Wk, bk, Wq, bq, slot_keys, scale, out_0, out_1
+):
+    nc = tc.nc
+    weights = {"k": Wk, "q": Wq}
+    biases = {"k": bk, "q": bq}
+    outputs = {"k": out_0, "q": out_1}
+
+    with ExitStack() as ctx:
+        keep = ctx.enter_context(tc.tile_pool(name="keep", bufs=1))
+        psum = ctx.enter_context(tc.psum_pool(name="psum", bufs=1))
+
+        x_rows = keep.tile([S, D], BF16)
+        nc.sync.dma_start(out=x_rows[:], in_=x.flatten_outer_dims())
+        slot_rows = keep.tile([P, SLOT_TILES, E], BF16)
+        nc.sync.dma_start(
+            out=slot_rows[:], in_=slot_keys.rearrange("(h n) e -> n h e", n=P)
+        )
+        w_rows = {}
+        for name in ("k", "q"):
+            for g in range(D_PASSES):
+                w_rows[name, g] = keep.tile([P, PACK, E], BF16, name="w_rows_%s%d" % (name, g))
+                nc.sync.dma_start(
+                    out=w_rows[name, g][:],
+                    in_=weights[name][g * K_PASS : (g + 1) * K_PASS, :].rearrange(
+                        "(p j) e -> p j e", j=PACK
+                    ),
+                )
+
+        scale_bf16 = keep.tile([P, 1], BF16)
+        bias = {}
+        with nc.allow_non_contiguous_dma(reason="a few bytes for each partition"):
+            nc.scalar.dma_start(out=scale_bf16[:], in_=scale.partition_broadcast(P))
+            for name in ("k", "q"):
+                bias[name] = keep.tile([P, E_TILES], BF16, name="bias_%s" % name)
+                nc.scalar.dma_start(
+                    out=bias[name][:], in_=biases[name].rearrange("(m t) -> m t", t=E_TILES)
+                )
+
+        warm = keep.tile([P, 1], F32)
+        nc.vector.memset(warm[:], 0.0)
+        nc.scalar.activation(out=warm[:], in_=warm[:], func=ACT.Exp)
+
+        ident = keep.tile([P, P], F32)
+        make_identity(nc, ident[:])
+
+        x_bank = psum.tile([P, D_PASSES, HALVES, S], F32)
+        for g in range(D_PASSES):
+            transpose_every_second_word(
+                nc, x_bank[:, g], x_rows[:, g * K_PASS : (g + 1) * K_PASS], ident[:]
+            )
+        x_grouped = keep.tile([P, D_PASSES * S * PACK], BF16, align_bytes=64)
+        nc.vector.tensor_copy(
+            out=x_grouped[:].bitcast(F32).rearrange("p (g s u) -> p g s u", g=D_PASSES, u=HALVES),
+            in_=x_bank[:].rearrange("p g u s -> p g s u"),
+        )
+        x_codes = keep.tile([P, D_PASSES, S], U32, align_bytes=64)
+        x_scales = keep.tile([P, D_PASSES, S], U8, align_bytes=64)
+        nc.vector.quantize_mx(
+            out=x_codes[:].rearrange("p g s -> p (g s)").bitcast(FP8X4),
+            scales=x_scales[:].rearrange("p g s -> p (g s)"),
+            in_=x_grouped[:],
+        )
+
+        slot_bank = psum.tile([P, HALVES, NS], F32)
+        for h in range(SLOT_TILES):
+            transpose_every_second_word(
+                nc, slot_bank[:, :, h * P : (h + 1) * P], slot_rows[:, h, :], ident[:]
+            )
+        slot_grouped = keep.tile([P, NS * PACK], BF16, align_bytes=64)
+        nc.scalar.copy(
+            out=slot_grouped[:].bitcast(F32).rearrange("p (n u) -> p n u", u=HALVES),
+            in_=slot_bank[:].rearrange("p u n -> p n u"),
+        )
+        slot_codes = keep.tile([P, NS], U32, align_bytes=64)
+        slot_scales = keep.tile([P, NS], U8, align_bytes=64)
+        nc.vector.quantize_mx(
+            out=slot_codes[:].bitcast(FP8X4), scales=slot_scales[:], in_=slot_grouped[:]
+        )
+
+        neg_scale = keep.tile([P, 1], F32)
+        nc.vector.tensor_scalar(
+            out=neg_scale[:], in0=scale_bf16[:], scalar1=-1.0, scalar2=None, op0=ALU.mult
+        )
+
+        scores = {}
+        for name in ("k", "q"):
+            w_codes = keep.tile([P, D_PASSES, E], U32, name="w_codes_%s" % name, align_bytes=64)
+            w_scales = keep.tile([P, D_PASSES, E], U8, name="w_scales_%s" % name, align_bytes=64)
+            for g in range(D_PASSES):
+                sorted_rows = w_rows[name, g][:].rearrange("p j (m t) -> p t m j", t=E_TILES)
+                w_grouped = keep.tile(
+                    [P, E_TILES, P, PACK], BF16, name="w_grouped_%s%d" % (name, g), align_bytes=64
+                )
+                nc.vector.tensor_copy(out=w_grouped[:, 0:2], in_=sorted_rows[:, 0:2])
+                nc.scalar.copy(out=w_grouped[:, 2:4], in_=sorted_rows[:, 2:4])
+                nc.vector.quantize_mx(
+                    out=w_codes[:, g, :].bitcast(FP8X4),
+                    scales=w_scales[:, g, :],
+                    in_=w_grouped[:].rearrange("p t m j -> p (t m j)"),
+                )
+
+            proj = psum.tile([P, E_TILES, S], F32, name="proj_%s" % name)
+            for t in range(E_TILES):
+                for g in range(D_PASSES):
+                    nc.tensor.matmul_mx(
+                        out=proj[:, t, :],
+                        lhsT=w_codes[:, g, t * P : (t + 1) * P].bitcast(FP8X4),
+                        lhsT_scale=w_scales[:, g, t * P : (t + 1) * P],
+                        rhs=x_codes[:, g, :].bitcast(FP8X4),
+                        rhs_scale=x_scales[:, g, :],
+                        start=(g == 0),
+                        stop=(g == D_PASSES - 1),
+                    )
+
+            key_grouped = keep.tile([P, S, PACK], BF16, name="key_grouped_%s" % name, align_bytes=64)
+            nc.vector.tensor_tensor(
+                out=key_grouped[:],
+                in0=proj[:].rearrange("m t s -> m s t"),
+                in1=bias[name][:].unsqueeze(1).to_broadcast([P, S, E_TILES]),
+                op=ALU.add,
+            )
+            key_codes = keep.tile([P, S], U32, name="key_codes_%s" % name, align_bytes=64)
+            key_scales = keep.tile([P, S], U8, name="key_scales_%s" % name, align_bytes=64)
+            nc.vector.quantize_mx(
+                out=key_codes[:].bitcast(FP8X4),
+                scales=key_scales[:],
+                in_=key_grouped[:].rearrange("m s t -> m (s t)"),
+            )
+
+            scores[name] = psum.tile([S, NS], F32, name="scores_%s" % name)
+            nc.tensor.matmul_mx(
+                out=scores[name][:],
+                lhsT=key_codes[:].bitcast(FP8X4),
+                lhsT_scale=key_scales[:],
+                rhs=slot_codes[:].bitcast(FP8X4),
+                rhs_scale=slot_scales[:],
+                start=True,
+                stop=True,
+            )
+
+        for name in ("k", "q"):
+            neg_z = keep.tile([S, NS], F32, name="neg_z_%s" % name)
+            neg_max = keep.tile([S, 1], F32, name="neg_max_%s" % name)
+            nc.vector.tensor_scalar(
+                out=neg_z[:],
+                in0=scores[name][:],
+                scalar1=neg_scale[:, 0:1],
+                scalar2=None,
+                op0=ALU.mult,
+                op1=ALU.min,
+                accum_out=neg_max[:],
+            )
+            exp_z = keep.tile([S, NS], F32, name="exp_z_%s" % name)
+            total = keep.tile([S, 1], F32, name="total_%s" % name)
+            nc.scalar.activation(
+                out=exp_z[:],
+                in_=neg_z[:],
+                func=ACT.Exp,
+                bias=neg_max[:, 0:1],
+                scale=-1.0,
+                accum_out=total[:],
+            )
+            inverse = keep.tile([S, 1], F32, name="inverse_%s" % name)
+            nc.vector.reciprocal(out=inverse[:], in_=total[:])
+            weights_out = keep.tile([S, NS], F32, name="weights_out_%s" % name)
+            nc.vector.tensor_scalar(
+                out=weights_out[:], in0=exp_z[:], scalar1=inverse[:, 0:1], scalar2=None, op0=ALU.mult
+            )
+            nc.sync.dma_start(out=outputs[name].flatten_outer_dims(), in_=weights_out[:])

@@ -38,9 +38,12 @@ def tile_slotmemoryphasor_pa_s_kernel(
     biases = {"k": bk, "q": bq}
     outputs = {"k": out_0, "q": out_1}
 
+    chunks = [(name, g) for name in ("k", "q") for g in range(D_PASSES)]
+
     with ExitStack() as ctx:
         keep = ctx.enter_context(tc.tile_pool(name="keep", bufs=1))
         psum = ctx.enter_context(tc.psum_pool(name="psum", bufs=1))
+        ctx.enter_context(tc.manual_schedule())
 
         x_rows = keep.tile([S, D], BF16)
         nc.sync.dma_start(out=x_rows[:], in_=x.flatten_outer_dims())
@@ -49,25 +52,24 @@ def tile_slotmemoryphasor_pa_s_kernel(
             out=slot_rows[:], in_=slot_keys.rearrange("(h n) e -> n h e", n=P)
         )
         w_rows = {}
-        for name in ("k", "q"):
-            for g in range(D_PASSES):
-                w_rows[name, g] = keep.tile([P, PACK, E], BF16, name="w_rows_%s%d" % (name, g))
-                nc.sync.dma_start(
-                    out=w_rows[name, g][:],
-                    in_=weights[name][g * K_PASS : (g + 1) * K_PASS, :].rearrange(
-                        "(p j) e -> p j e", j=PACK
-                    ),
-                )
+        for name, g in chunks:
+            w_rows[name, g] = keep.tile([P, PACK, E], BF16, name="w_rows_%s%d" % (name, g))
+            nc.sync.dma_start(
+                out=w_rows[name, g][:],
+                in_=weights[name][g * K_PASS : (g + 1) * K_PASS, :].rearrange(
+                    "(p j) e -> p j e", j=PACK
+                ),
+            )
 
         scale_bf16 = keep.tile([P, 1], BF16)
         bias = {}
         with nc.allow_non_contiguous_dma(reason="a few bytes for each partition"):
-            nc.scalar.dma_start(out=scale_bf16[:], in_=scale.partition_broadcast(P))
             for name in ("k", "q"):
                 bias[name] = keep.tile([P, E_TILES], BF16, name="bias_%s" % name)
                 nc.scalar.dma_start(
                     out=bias[name][:], in_=biases[name].rearrange("(m t) -> m t", t=E_TILES)
                 )
+            nc.scalar.dma_start(out=scale_bf16[:], in_=scale.partition_broadcast(P))
 
         warm = keep.tile([P, 1], F32)
         nc.vector.memset(warm[:], 0.0)
@@ -75,6 +77,9 @@ def tile_slotmemoryphasor_pa_s_kernel(
 
         ident = keep.tile([P, P], F32)
         make_identity(nc, ident[:])
+
+        def quantise(codes, scales, grouped):
+            nc.vector.quantize_mx(out=codes.bitcast(FP8X4), scales=scales, in_=grouped)
 
         x_bank = psum.tile([P, D_PASSES, HALVES, S], F32)
         for g in range(D_PASSES):
@@ -88,10 +93,10 @@ def tile_slotmemoryphasor_pa_s_kernel(
         )
         x_codes = keep.tile([P, D_PASSES, S], U32, align_bytes=64)
         x_scales = keep.tile([P, D_PASSES, S], U8, align_bytes=64)
-        nc.vector.quantize_mx(
-            out=x_codes[:].rearrange("p g s -> p (g s)").bitcast(FP8X4),
-            scales=x_scales[:].rearrange("p g s -> p (g s)"),
-            in_=x_grouped[:],
+        quantise(
+            x_codes[:].rearrange("p g s -> p (g s)"),
+            x_scales[:].rearrange("p g s -> p (g s)"),
+            x_grouped[:],
         )
 
         slot_bank = psum.tile([P, HALVES, NS], F32)
@@ -106,59 +111,65 @@ def tile_slotmemoryphasor_pa_s_kernel(
         )
         slot_codes = keep.tile([P, NS], U32, align_bytes=64)
         slot_scales = keep.tile([P, NS], U8, align_bytes=64)
-        nc.vector.quantize_mx(
-            out=slot_codes[:].bitcast(FP8X4), scales=slot_scales[:], in_=slot_grouped[:]
-        )
 
-        neg_scale = keep.tile([P, 1], F32)
-        nc.vector.tensor_scalar(
-            out=neg_scale[:], in0=scale_bf16[:], scalar1=-1.0, scalar2=None, op0=ALU.mult
-        )
-
-        scores = {}
+        w_codes = {}
+        w_scales = {}
         for name in ("k", "q"):
-            w_codes = keep.tile([P, D_PASSES, E], U32, name="w_codes_%s" % name, align_bytes=64)
-            w_scales = keep.tile([P, D_PASSES, E], U8, name="w_scales_%s" % name, align_bytes=64)
-            for g in range(D_PASSES):
-                sorted_rows = w_rows[name, g][:].rearrange("p j (m t) -> p t m j", t=E_TILES)
-                w_grouped = keep.tile(
-                    [P, E_TILES, P, PACK], BF16, name="w_grouped_%s%d" % (name, g), align_bytes=64
-                )
-                nc.vector.tensor_copy(out=w_grouped[:, 0:2], in_=sorted_rows[:, 0:2])
-                nc.scalar.copy(out=w_grouped[:, 2:4], in_=sorted_rows[:, 2:4])
-                nc.vector.quantize_mx(
-                    out=w_codes[:, g, :].bitcast(FP8X4),
-                    scales=w_scales[:, g, :],
-                    in_=w_grouped[:].rearrange("p t m j -> p (t m j)"),
-                )
+            w_codes[name] = keep.tile([P, D_PASSES, E], U32, name="w_codes_%s" % name, align_bytes=64)
+            w_scales[name] = keep.tile([P, D_PASSES, E], U8, name="w_scales_%s" % name, align_bytes=64)
+        by_vector = slice(0, E_TILES // 2)
+        by_scalar = slice(E_TILES // 2, E_TILES)
+        from_scalar = (slot_codes[:], slot_scales[:], slot_grouped[:])
+        for name, g in chunks:
+            sorted_rows = w_rows[name, g][:].rearrange("p j (m t) -> p t m j", t=E_TILES)
+            w_grouped = keep.tile(
+                [P, E_TILES, P, PACK], BF16, name="w_grouped_%s%d" % (name, g), align_bytes=64
+            )
+            codes = w_codes[name][:, g, :].rearrange("p (t m) -> p t m", t=E_TILES)
+            scales = w_scales[name][:, g, :].rearrange("p (t m) -> p t m", t=E_TILES)
+            nc.vector.tensor_copy(out=w_grouped[:, by_vector], in_=sorted_rows[:, by_vector])
+            nc.scalar.copy(out=w_grouped[:, by_scalar], in_=sorted_rows[:, by_scalar])
+            quantise(*from_scalar)
+            quantise(
+                codes[:, by_vector].rearrange("p t m -> p (t m)"),
+                scales[:, by_vector].rearrange("p t m -> p (t m)"),
+                w_grouped[:, by_vector].rearrange("p t m j -> p (t m j)"),
+            )
+            from_scalar = (
+                codes[:, by_scalar].rearrange("p t m -> p (t m)"),
+                scales[:, by_scalar].rearrange("p t m -> p (t m)"),
+                w_grouped[:, by_scalar].rearrange("p t m j -> p (t m j)"),
+            )
+        quantise(*from_scalar)
 
-            proj = psum.tile([P, E_TILES, S], F32, name="proj_%s" % name)
+        proj = {}
+        for name in ("k", "q"):
+            proj[name] = psum.tile([P, E_TILES, S], F32, name="proj_%s" % name)
             for t in range(E_TILES):
                 for g in range(D_PASSES):
                     nc.tensor.matmul_mx(
-                        out=proj[:, t, :],
-                        lhsT=w_codes[:, g, t * P : (t + 1) * P].bitcast(FP8X4),
-                        lhsT_scale=w_scales[:, g, t * P : (t + 1) * P],
+                        out=proj[name][:, t, :],
+                        lhsT=w_codes[name][:, g, t * P : (t + 1) * P].bitcast(FP8X4),
+                        lhsT_scale=w_scales[name][:, g, t * P : (t + 1) * P],
                         rhs=x_codes[:, g, :].bitcast(FP8X4),
                         rhs_scale=x_scales[:, g, :],
                         start=(g == 0),
                         stop=(g == D_PASSES - 1),
                     )
 
+        neg_scale = keep.tile([P, 1], F32)
+        scores = {}
+        for name in ("k", "q"):
             key_grouped = keep.tile([P, S, PACK], BF16, name="key_grouped_%s" % name, align_bytes=64)
             nc.vector.tensor_tensor(
                 out=key_grouped[:],
-                in0=proj[:].rearrange("m t s -> m s t"),
+                in0=proj[name][:].rearrange("m t s -> m s t"),
                 in1=bias[name][:].unsqueeze(1).to_broadcast([P, S, E_TILES]),
                 op=ALU.add,
             )
             key_codes = keep.tile([P, S], U32, name="key_codes_%s" % name, align_bytes=64)
             key_scales = keep.tile([P, S], U8, name="key_scales_%s" % name, align_bytes=64)
-            nc.vector.quantize_mx(
-                out=key_codes[:].bitcast(FP8X4),
-                scales=key_scales[:],
-                in_=key_grouped[:].rearrange("m s t -> m (s t)"),
-            )
+            quantise(key_codes[:], key_scales[:], key_grouped[:].rearrange("m s t -> m (s t)"))
 
             scores[name] = psum.tile([S, NS], F32, name="scores_%s" % name)
             nc.tensor.matmul_mx(
@@ -171,25 +182,31 @@ def tile_slotmemoryphasor_pa_s_kernel(
                 stop=True,
             )
 
+        nc.vector.tensor_scalar(
+            out=neg_scale[:], in0=scale_bf16[:], scalar1=-1.0, scalar2=None, op0=ALU.mult
+        )
+        neg_z = {}
+        neg_max = {}
         for name in ("k", "q"):
-            neg_z = keep.tile([S, NS], F32, name="neg_z_%s" % name)
-            neg_max = keep.tile([S, 1], F32, name="neg_max_%s" % name)
+            neg_z[name] = keep.tile([S, NS], F32, name="neg_z_%s" % name)
+            neg_max[name] = keep.tile([S, 1], F32, name="neg_max_%s" % name)
             nc.vector.tensor_scalar(
-                out=neg_z[:],
+                out=neg_z[name][:],
                 in0=scores[name][:],
                 scalar1=neg_scale[:, 0:1],
                 scalar2=None,
                 op0=ALU.mult,
                 op1=ALU.min,
-                accum_out=neg_max[:],
+                accum_out=neg_max[name][:],
             )
+        for name in ("k", "q"):
             exp_z = keep.tile([S, NS], F32, name="exp_z_%s" % name)
             total = keep.tile([S, 1], F32, name="total_%s" % name)
             nc.scalar.activation(
                 out=exp_z[:],
-                in_=neg_z[:],
+                in_=neg_z[name][:],
                 func=ACT.Exp,
-                bias=neg_max[:, 0:1],
+                bias=neg_max[name][:, 0:1],
                 scale=-1.0,
                 accum_out=total[:],
             )

@@ -117,30 +117,31 @@ def tile_slotmemoryphasor_pa_s_kernel(
         for name in ("k", "q"):
             w_codes[name] = keep.tile([P, D_PASSES, E], U32, name="w_codes_%s" % name, align_bytes=64)
             w_scales[name] = keep.tile([P, D_PASSES, E], U8, name="w_scales_%s" % name, align_bytes=64)
-        by_vector = slice(0, E_TILES // 2)
-        by_scalar = slice(E_TILES // 2, E_TILES)
-        from_scalar = (slot_codes[:], slot_scales[:], slot_grouped[:])
+        by_vector = slice(0, P // 2)
+        by_scalar = slice(P // 2, P)
+        half = E // 2
+        one_step_late = [(slot_codes[:], slot_scales[:], slot_grouped[:])]
         for name, g in chunks:
-            sorted_rows = w_rows[name, g][:].rearrange("p j (m t) -> p t m j", t=E_TILES)
             w_grouped = keep.tile(
                 [P, E_TILES, P, PACK], BF16, name="w_grouped_%s%d" % (name, g), align_bytes=64
             )
-            codes = w_codes[name][:, g, :].rearrange("p (t m) -> p t m", t=E_TILES)
-            scales = w_scales[name][:, g, :].rearrange("p (t m) -> p t m", t=E_TILES)
-            nc.vector.tensor_copy(out=w_grouped[:, by_vector], in_=sorted_rows[:, by_vector])
-            nc.scalar.copy(out=w_grouped[:, by_scalar], in_=sorted_rows[:, by_scalar])
-            quantise(*from_scalar)
-            quantise(
-                codes[:, by_vector].rearrange("p t m -> p (t m)"),
-                scales[:, by_vector].rearrange("p t m -> p (t m)"),
-                w_grouped[:, by_vector].rearrange("p t m j -> p (t m j)"),
-            )
-            from_scalar = (
-                codes[:, by_scalar].rearrange("p t m -> p (t m)"),
-                scales[:, by_scalar].rearrange("p t m -> p (t m)"),
-                w_grouped[:, by_scalar].rearrange("p t m j -> p (t m j)"),
-            )
-        quantise(*from_scalar)
+            source = w_rows[name, g][:].rearrange("p j (m t) -> p m j t", t=E_TILES)
+            target = w_grouped[:].rearrange("p t m j -> p m j t")
+            nc.vector.tensor_copy(out=target[:, by_vector], in_=source[:, by_vector])
+            nc.scalar.copy(out=target[:, by_scalar], in_=source[:, by_scalar])
+            for job in one_step_late:
+                quantise(*job)
+            flat = w_grouped[:].rearrange("p t m j -> p (t m j)")
+            one_step_late = [
+                (
+                    w_codes[name][:, g, c : c + half],
+                    w_scales[name][:, g, c : c + half],
+                    flat[:, c * PACK : (c + half) * PACK],
+                )
+                for c in range(0, E, half)
+            ]
+        for job in one_step_late:
+            quantise(*job)
 
         proj = {}
         for name in ("k", "q"):

@@ -47,10 +47,6 @@ def tile_slotmemoryphasor_pa_s_kernel(
 
         x_rows = keep.tile([S, D], BF16)
         nc.sync.dma_start(out=x_rows[:], in_=x.flatten_outer_dims())
-        slot_rows = keep.tile([P, SLOT_TILES, E], BF16)
-        nc.sync.dma_start(
-            out=slot_rows[:], in_=slot_keys.rearrange("(h n) e -> n h e", n=P)
-        )
         w_rows = {}
         for name, g in chunks:
             w_rows[name, g] = keep.tile([P, PACK, E], BF16, name="w_rows_%s%d" % (name, g))
@@ -60,6 +56,10 @@ def tile_slotmemoryphasor_pa_s_kernel(
                     "(p j) e -> p j e", j=PACK
                 ),
             )
+        slot_rows = keep.tile([P, SLOT_TILES, E], BF16)
+        nc.sync.dma_start(
+            out=slot_rows[:], in_=slot_keys.rearrange("(h n) e -> n h e", n=P)
+        )
 
         scale_bf16 = keep.tile([P, 1], BF16)
         bias = {}
@@ -99,19 +99,6 @@ def tile_slotmemoryphasor_pa_s_kernel(
             x_grouped[:],
         )
 
-        slot_bank = psum.tile([P, HALVES, NS], F32)
-        for h in range(SLOT_TILES):
-            transpose_every_second_word(
-                nc, slot_bank[:, :, h * P : (h + 1) * P], slot_rows[:, h, :], ident[:]
-            )
-        slot_grouped = keep.tile([P, NS * PACK], BF16, align_bytes=64)
-        nc.scalar.copy(
-            out=slot_grouped[:].bitcast(F32).rearrange("p (n u) -> p n u", u=HALVES),
-            in_=slot_bank[:].rearrange("p u n -> p n u"),
-        )
-        slot_codes = keep.tile([P, NS], U32, align_bytes=64)
-        slot_scales = keep.tile([P, NS], U8, align_bytes=64)
-
         w_codes = {}
         w_scales = {}
         for name in ("k", "q"):
@@ -120,7 +107,7 @@ def tile_slotmemoryphasor_pa_s_kernel(
         by_vector = slice(0, P // 2)
         by_scalar = slice(P // 2, P)
         half = E // 2
-        one_step_late = [(slot_codes[:], slot_scales[:], slot_grouped[:])]
+        one_step_late = []
         for name, g in chunks:
             w_grouped = keep.tile(
                 [P, E_TILES, P, PACK], BF16, name="w_grouped_%s%d" % (name, g), align_bytes=64
@@ -144,7 +131,8 @@ def tile_slotmemoryphasor_pa_s_kernel(
             quantise(*job)
 
         proj = {}
-        for name in ("k", "q"):
+
+        def project(name):
             proj[name] = psum.tile([P, E_TILES, S], F32, name="proj_%s" % name)
             for t in range(E_TILES):
                 for g in range(D_PASSES):
@@ -158,20 +146,42 @@ def tile_slotmemoryphasor_pa_s_kernel(
                         stop=(g == D_PASSES - 1),
                     )
 
-        neg_scale = keep.tile([P, 1], F32)
-        scores = {}
-        for name in ("k", "q"):
-            key_grouped = keep.tile([P, S, PACK], BF16, name="key_grouped_%s" % name, align_bytes=64)
+        project("k")
+
+        slot_bank = psum.tile([P, HALVES, NS], F32)
+        for h in range(SLOT_TILES):
+            transpose_every_second_word(
+                nc, slot_bank[:, :, h * P : (h + 1) * P], slot_rows[:, h, :], ident[:]
+            )
+        slot_grouped = keep.tile([P, NS * PACK], BF16, align_bytes=64)
+        nc.scalar.copy(
+            out=slot_grouped[:].bitcast(F32).rearrange("p (n u) -> p n u", u=HALVES),
+            in_=slot_bank[:].rearrange("p u n -> p n u"),
+        )
+        slot_codes = keep.tile([P, NS], U32, align_bytes=64)
+        slot_scales = keep.tile([P, NS], U8, align_bytes=64)
+
+        project("q")
+
+        key_grouped = {}
+
+        def add_bias(name):
+            key_grouped[name] = keep.tile(
+                [P, S, PACK], BF16, name="key_grouped_%s" % name, align_bytes=64
+            )
             nc.vector.tensor_tensor(
-                out=key_grouped[:],
+                out=key_grouped[name][:],
                 in0=proj[name][:].rearrange("m t s -> m s t"),
                 in1=bias[name][:].unsqueeze(1).to_broadcast([P, S, E_TILES]),
                 op=ALU.add,
             )
+
+        scores = {}
+
+        def score(name):
             key_codes = keep.tile([P, S], U32, name="key_codes_%s" % name, align_bytes=64)
             key_scales = keep.tile([P, S], U8, name="key_scales_%s" % name, align_bytes=64)
-            quantise(key_codes[:], key_scales[:], key_grouped[:].rearrange("m s t -> m (s t)"))
-
+            quantise(key_codes[:], key_scales[:], key_grouped[name][:].rearrange("m s t -> m (s t)"))
             scores[name] = psum.tile([S, NS], F32, name="scores_%s" % name)
             nc.tensor.matmul_mx(
                 out=scores[name][:],
@@ -183,6 +193,13 @@ def tile_slotmemoryphasor_pa_s_kernel(
                 stop=True,
             )
 
+        add_bias("k")
+        quantise(slot_codes[:], slot_scales[:], slot_grouped[:])
+        score("k")
+        add_bias("q")
+        score("q")
+
+        neg_scale = keep.tile([P, 1], F32)
         nc.vector.tensor_scalar(
             out=neg_scale[:], in0=scale_bf16[:], scalar1=-1.0, scalar2=None, op0=ALU.mult
         )

@@ -20,6 +20,7 @@ S, D, E, NS = 128, 1024, 512, 256
 D_PASSES = D // K_PASS
 E_TILES = E // P
 SLOT_TILES = NS // P
+WARM_PASSES = 2
 
 FLOPS = 2 * (2 * S * D * E) + 2 * (2 * S * E * NS)
 
@@ -87,17 +88,12 @@ def tile_slotmemoryphasor_pa_s_kernel(
                 nc, x_bank[:, g], x_rows[:, g * K_PASS : (g + 1) * K_PASS], ident[:]
             )
         x_grouped = keep.tile([P, D_PASSES * S * PACK], BF16, align_bytes=64)
-        nc.vector.tensor_copy(
+        nc.scalar.copy(
             out=x_grouped[:].bitcast(F32).rearrange("p (g s u) -> p g s u", g=D_PASSES, u=HALVES),
             in_=x_bank[:].rearrange("p g u s -> p g s u"),
         )
         x_codes = keep.tile([P, D_PASSES, S], U32, align_bytes=64)
         x_scales = keep.tile([P, D_PASSES, S], U8, align_bytes=64)
-        quantise(
-            x_codes[:].rearrange("p g s -> p (g s)"),
-            x_scales[:].rearrange("p g s -> p (g s)"),
-            x_grouped[:],
-        )
 
         w_codes = {}
         w_scales = {}
@@ -107,7 +103,13 @@ def tile_slotmemoryphasor_pa_s_kernel(
         by_vector = slice(0, P // 2)
         by_scalar = slice(P // 2, P)
         half = E // 2
-        one_step_late = []
+        one_step_late = [
+            (
+                x_codes[:].rearrange("p g s -> p (g s)"),
+                x_scales[:].rearrange("p g s -> p (g s)"),
+                x_grouped[:],
+            )
+        ]
         for name, g in chunks:
             w_grouped = keep.tile(
                 [P, E_TILES, P, PACK], BF16, name="w_grouped_%s%d" % (name, g), align_bytes=64
@@ -146,6 +148,21 @@ def tile_slotmemoryphasor_pa_s_kernel(
                         stop=(g == D_PASSES - 1),
                     )
 
+        unread_bank = psum.tile([S, E], F32)
+
+        def keep_busy(name):
+            for repeat in range(WARM_PASSES):
+                nc.tensor.matmul_mx(
+                    out=unread_bank[:],
+                    lhsT=x_codes[:, 0, :].bitcast(FP8X4),
+                    lhsT_scale=x_scales[:, 0, :],
+                    rhs=w_codes[name][:, 0, :].bitcast(FP8X4),
+                    rhs_scale=w_scales[name][:, 0, :],
+                    start=True,
+                    stop=True,
+                )
+
+        keep_busy("k")
         project("k")
 
         slot_bank = psum.tile([P, HALVES, NS], F32)
@@ -161,6 +178,7 @@ def tile_slotmemoryphasor_pa_s_kernel(
         slot_codes = keep.tile([P, NS], U32, align_bytes=64)
         slot_scales = keep.tile([P, NS], U8, align_bytes=64)
 
+        keep_busy("q")
         project("q")
 
         key_grouped = {}
@@ -197,12 +215,12 @@ def tile_slotmemoryphasor_pa_s_kernel(
         quantise(slot_codes[:], slot_scales[:], slot_grouped[:])
         score("k")
         add_bias("q")
-        score("q")
-
         neg_scale = keep.tile([P, 1], F32)
         nc.vector.tensor_scalar(
             out=neg_scale[:], in0=scale_bf16[:], scalar1=-1.0, scalar2=None, op0=ALU.mult
         )
+        score("q")
+
         neg_z = {}
         neg_max = {}
         for name in ("k", "q"):

@@ -67,10 +67,10 @@ def tile_slotmemoryphasor_pa_s_kernel(
         with nc.allow_non_contiguous_dma(reason="a few bytes for each partition"):
             for name in ("k", "q"):
                 bias[name] = keep.tile([P, E_TILES], BF16, name="bias_%s" % name)
-                nc.scalar.dma_start(
+                nc.sync.dma_start(
                     out=bias[name][:], in_=biases[name].rearrange("(m t) -> m t", t=E_TILES)
                 )
-            nc.scalar.dma_start(out=scale_bf16[:], in_=scale.partition_broadcast(P))
+            nc.sync.dma_start(out=scale_bf16[:], in_=scale.partition_broadcast(P))
 
         warm = keep.tile([P, 1], F32)
         nc.vector.memset(warm[:], 0.0)

@@ -47,7 +47,6 @@ def tile_slotmemoryphasor_pa_s_kernel(
         ctx.enter_context(tc.manual_schedule())
 
         x_rows = keep.tile([S, D], BF16)
-        nc.sync.dma_start(out=x_rows[:], in_=x.flatten_outer_dims())
         w_rows = {}
         for name, g in chunks:
             w_rows[name, g] = keep.tile([P, PACK, E], BF16, name="w_rows_%s%d" % (name, g))
@@ -57,6 +56,8 @@ def tile_slotmemoryphasor_pa_s_kernel(
                     "(p j) e -> p j e", j=PACK
                 ),
             )
+            if (name, g) == chunks[0]:
+                nc.sync.dma_start(out=x_rows[:], in_=x.flatten_outer_dims())
         slot_rows = keep.tile([P, SLOT_TILES, E], BF16)
         nc.sync.dma_start(
             out=slot_rows[:], in_=slot_keys.rearrange("(h n) e -> n h e", n=P)
@@ -88,10 +89,6 @@ def tile_slotmemoryphasor_pa_s_kernel(
                 nc, x_bank[:, g], x_rows[:, g * K_PASS : (g + 1) * K_PASS], ident[:]
             )
         x_grouped = keep.tile([P, D_PASSES * S * PACK], BF16, align_bytes=64)
-        nc.scalar.copy(
-            out=x_grouped[:].bitcast(F32).rearrange("p (g s u) -> p g s u", g=D_PASSES, u=HALVES),
-            in_=x_bank[:].rearrange("p g u s -> p g s u"),
-        )
         x_codes = keep.tile([P, D_PASSES, S], U32, align_bytes=64)
         x_scales = keep.tile([P, D_PASSES, S], U8, align_bytes=64)
 
@@ -103,13 +100,12 @@ def tile_slotmemoryphasor_pa_s_kernel(
         by_vector = slice(0, P // 2)
         by_scalar = slice(P // 2, P)
         half = E // 2
-        one_step_late = [
-            (
-                x_codes[:].rearrange("p g s -> p (g s)"),
-                x_scales[:].rearrange("p g s -> p (g s)"),
-                x_grouped[:],
-            )
-        ]
+        x_job = (
+            x_codes[:].rearrange("p g s -> p (g s)"),
+            x_scales[:].rearrange("p g s -> p (g s)"),
+            x_grouped[:],
+        )
+        one_step_late = []
         for name, g in chunks:
             w_grouped = keep.tile(
                 [P, E_TILES, P, PACK], BF16, name="w_grouped_%s%d" % (name, g), align_bytes=64
@@ -129,6 +125,16 @@ def tile_slotmemoryphasor_pa_s_kernel(
                 )
                 for c in range(0, E, half)
             ]
+            if (name, g) == chunks[0]:
+                nc.scalar.copy(
+                    out=x_grouped[:]
+                    .bitcast(F32)
+                    .rearrange("p (g s u) -> p g s u", g=D_PASSES, u=HALVES),
+                    in_=x_bank[:].rearrange("p g u s -> p g s u"),
+                )
+                for job in one_step_late:
+                    quantise(*job)
+                one_step_late = [x_job]
         for job in one_step_late:
             quantise(*job)
 

@@ -97,8 +97,8 @@ def tile_slotmemoryphasor_pa_s_kernel(
         for name in ("k", "q"):
             w_codes[name] = keep.tile([P, D_PASSES, E], U32, name="w_codes_%s" % name, align_bytes=64)
             w_scales[name] = keep.tile([P, D_PASSES, E], U8, name="w_scales_%s" % name, align_bytes=64)
-        by_vector = slice(0, P // 2)
-        by_scalar = slice(P // 2, P)
+        by_vector = slice(0, E_TILES // 2)
+        by_scalar = slice(E_TILES // 2, E_TILES)
         half = E // 2
         x_job = (
             x_codes[:].rearrange("p g s -> p (g s)"),
@@ -112,12 +112,10 @@ def tile_slotmemoryphasor_pa_s_kernel(
             )
             source = w_rows[name, g][:].rearrange("p j (m t) -> p m j t", t=E_TILES)
             target = w_grouped[:].rearrange("p t m j -> p m j t")
-            nc.vector.tensor_copy(out=target[:, by_vector], in_=source[:, by_vector])
-            nc.scalar.copy(out=target[:, by_scalar], in_=source[:, by_scalar])
-            for job in one_step_late:
-                quantise(*job)
+            nc.vector.tensor_copy(out=target[:, :, :, by_vector], in_=source[:, :, :, by_vector])
+            nc.scalar.copy(out=target[:, :, :, by_scalar], in_=source[:, :, :, by_scalar])
             flat = w_grouped[:].rearrange("p t m j -> p (t m j)")
-            one_step_late = [
+            vector_half, scalar_half = [
                 (
                     w_codes[name][:, g, c : c + half],
                     w_scales[name][:, g, c : c + half],
@@ -125,6 +123,10 @@ def tile_slotmemoryphasor_pa_s_kernel(
                 )
                 for c in range(0, E, half)
             ]
+            for job in one_step_late:
+                quantise(*job)
+            quantise(*vector_half)
+            one_step_late = [scalar_half]
             if (name, g) == chunks[0]:
                 nc.scalar.copy(
                     out=x_grouped[:]
@@ -132,9 +134,7 @@ def tile_slotmemoryphasor_pa_s_kernel(
                     .rearrange("p (g s u) -> p g s u", g=D_PASSES, u=HALVES),
                     in_=x_bank[:].rearrange("p g u s -> p g s u"),
                 )
-                for job in one_step_late:
-                    quantise(*job)
-                one_step_late = [x_job]
+                one_step_late = [scalar_half, x_job]
         for job in one_step_late:
             quantise(*job)
 

@@ -169,7 +169,6 @@ def tile_slotmemoryphasor_pa_s_kernel(
                 )
 
         keep_busy("k")
-        project("k")
 
         slot_bank = psum.tile([P, HALVES, NS], F32)
         for h in range(SLOT_TILES):
@@ -184,7 +183,7 @@ def tile_slotmemoryphasor_pa_s_kernel(
         slot_codes = keep.tile([P, NS], U32, align_bytes=64)
         slot_scales = keep.tile([P, NS], U8, align_bytes=64)
 
-        keep_busy("q")
+        project("k")
         project("q")
 
         key_grouped = {}

@@ -20,7 +20,7 @@ S, D, E, NS = 128, 1024, 512, 256
 D_PASSES = D // K_PASS
 E_TILES = E // P
 SLOT_TILES = NS // P
-WARM_PASSES = 2
+WARM_PASSES = 6
 
 FLOPS = 2 * (2 * S * D * E) + 2 * (2 * S * E * NS)
 
@@ -47,6 +47,10 @@ def tile_slotmemoryphasor_pa_s_kernel(
         ctx.enter_context(tc.manual_schedule())
 
         x_rows = keep.tile([S, D], BF16)
+        x_flat = x.flatten_outer_dims()
+        for g in range(D_PASSES):
+            cols = slice(g * K_PASS, (g + 1) * K_PASS)
+            nc.sync.dma_start(out=x_rows[:, cols], in_=x_flat[:, cols])
         w_rows = {}
         for name, g in chunks:
             w_rows[name, g] = keep.tile([P, PACK, E], BF16, name="w_rows_%s%d" % (name, g))
@@ -56,8 +60,6 @@ def tile_slotmemoryphasor_pa_s_kernel(
                     "(p j) e -> p j e", j=PACK
                 ),
             )
-            if (name, g) == chunks[0]:
-                nc.sync.dma_start(out=x_rows[:], in_=x.flatten_outer_dims())
         slot_rows = keep.tile([P, SLOT_TILES, E], BF16)
         nc.sync.dma_start(
             out=slot_rows[:], in_=slot_keys.rearrange("(h n) e -> n h e", n=P)
@@ -83,14 +85,21 @@ def tile_slotmemoryphasor_pa_s_kernel(
         def quantise(codes, scales, grouped):
             nc.vector.quantize_mx(out=codes.bitcast(FP8X4), scales=scales, in_=grouped)
 
-        x_bank = psum.tile([P, D_PASSES, HALVES, S], F32)
+        x_banks = []
         for g in range(D_PASSES):
+            x_bank = psum.tile([P, HALVES, S], F32, name="x_bank_%d" % g)
             transpose_every_second_word(
-                nc, x_bank[:, g], x_rows[:, g * K_PASS : (g + 1) * K_PASS], ident[:]
+                nc, x_bank[:], x_rows[:, g * K_PASS : (g + 1) * K_PASS], ident[:]
             )
-        x_grouped = keep.tile([P, D_PASSES * S * PACK], BF16, align_bytes=64)
+            x_banks.append(x_bank)
+        x_grouped = keep.tile([P, D_PASSES, S * PACK], BF16, align_bytes=64)
         x_codes = keep.tile([P, D_PASSES, S], U32, align_bytes=64)
         x_scales = keep.tile([P, D_PASSES, S], U8, align_bytes=64)
+        for g in range(D_PASSES):
+            nc.vector.tensor_copy(
+                out=x_grouped[:, g, :].bitcast(F32).rearrange("p (s u) -> p s u", u=HALVES),
+                in_=x_banks[g][:].rearrange("p u s -> p s u"),
+            )
 
         w_codes = {}
         w_scales = {}
@@ -100,12 +109,13 @@ def tile_slotmemoryphasor_pa_s_kernel(
         by_vector = slice(0, E_TILES // 2)
         by_scalar = slice(E_TILES // 2, E_TILES)
         half = E // 2
-        x_job = (
-            x_codes[:].rearrange("p g s -> p (g s)"),
-            x_scales[:].rearrange("p g s -> p (g s)"),
-            x_grouped[:],
-        )
-        one_step_late = []
+        one_step_late = [
+            (
+                x_codes[:].rearrange("p g s -> p (g s)"),
+                x_scales[:].rearrange("p g s -> p (g s)"),
+                x_grouped[:].rearrange("p g c -> p (g c)"),
+            )
+        ]
         for name, g in chunks:
             w_grouped = keep.tile(
                 [P, E_TILES, P, PACK], BF16, name="w_grouped_%s%d" % (name, g), align_bytes=64
@@ -127,14 +137,6 @@ def tile_slotmemoryphasor_pa_s_kernel(
                 quantise(*job)
             quantise(*vector_half)
             one_step_late = [scalar_half]
-            if (name, g) == chunks[0]:
-                nc.scalar.copy(
-                    out=x_grouped[:]
-                    .bitcast(F32)
-                    .rearrange("p (g s u) -> p g s u", g=D_PASSES, u=HALVES),
-                    in_=x_bank[:].rearrange("p g u s -> p g s u"),
-                )
-                one_step_late = [scalar_half, x_job]
         for job in one_step_late:
             quantise(*job)
 
@@ -154,21 +156,19 @@ def tile_slotmemoryphasor_pa_s_kernel(
                         stop=(g == D_PASSES - 1),
                     )
 
-        unread_bank = psum.tile([S, E], F32)
+        unread_bank = psum.tile([S, D_PASSES * S], F32)
+        for repeat in range(WARM_PASSES):
+            nc.tensor.matmul_mx(
+                out=unread_bank[:],
+                lhsT=x_codes[:, 0, :].bitcast(FP8X4),
+                lhsT_scale=x_scales[:, 0, :],
+                rhs=x_codes[:].rearrange("p g s -> p (g s)").bitcast(FP8X4),
+                rhs_scale=x_scales[:].rearrange("p g s -> p (g s)"),
+                start=True,
+                stop=True,
+            )
 
-        def keep_busy(name):
-            for repeat in range(WARM_PASSES):
-                nc.tensor.matmul_mx(
-                    out=unread_bank[:],
-                    lhsT=x_codes[:, 0, :].bitcast(FP8X4),
-                    lhsT_scale=x_scales[:, 0, :],
-                    rhs=w_codes[name][:, 0, :].bitcast(FP8X4),
-                    rhs_scale=w_scales[name][:, 0, :],
-                    start=True,
-                    stop=True,
-                )
-
-        keep_busy("k")
+        project("k")
 
         slot_bank = psum.tile([P, HALVES, NS], F32)
         for h in range(SLOT_TILES):
@@ -183,28 +183,34 @@ def tile_slotmemoryphasor_pa_s_kernel(
         slot_codes = keep.tile([P, NS], U32, align_bytes=64)
         slot_scales = keep.tile([P, NS], U8, align_bytes=64)
 
-        project("k")
         project("q")
 
         key_grouped = {}
 
-        def add_bias(name):
+        def add_bias(name, parts):
             key_grouped[name] = keep.tile(
                 [P, S, PACK], BF16, name="key_grouped_%s" % name, align_bytes=64
             )
-            nc.vector.tensor_tensor(
-                out=key_grouped[name][:],
-                in0=proj[name][:].rearrange("m t s -> m s t"),
-                in1=bias[name][:].unsqueeze(1).to_broadcast([P, S, E_TILES]),
-                op=ALU.add,
-            )
+            for tokens in parts:
+                count = tokens.stop - tokens.start
+                nc.vector.tensor_tensor(
+                    out=key_grouped[name][:, tokens, :],
+                    in0=proj[name][:, :, tokens].rearrange("m t s -> m s t"),
+                    in1=bias[name][:].unsqueeze(1).to_broadcast([P, count, E_TILES]),
+                    op=ALU.add,
+                )
 
         scores = {}
 
-        def score(name):
+        def score(name, parts):
             key_codes = keep.tile([P, S], U32, name="key_codes_%s" % name, align_bytes=64)
             key_scales = keep.tile([P, S], U8, name="key_scales_%s" % name, align_bytes=64)
-            quantise(key_codes[:], key_scales[:], key_grouped[name][:].rearrange("m s t -> m (s t)"))
+            for tokens in parts:
+                quantise(
+                    key_codes[:, tokens],
+                    key_scales[:, tokens],
+                    key_grouped[name][:, tokens, :].rearrange("m s t -> m (s t)"),
+                )
             scores[name] = psum.tile([S, NS], F32, name="scores_%s" % name)
             nc.tensor.matmul_mx(
                 out=scores[name][:],
@@ -216,15 +222,17 @@ def tile_slotmemoryphasor_pa_s_kernel(
                 stop=True,
             )
 
-        add_bias("k")
+        whole = [slice(0, S)]
+        halves = [slice(0, S // 2), slice(S // 2, S)]
+        add_bias("k", whole)
         quantise(slot_codes[:], slot_scales[:], slot_grouped[:])
-        score("k")
-        add_bias("q")
         neg_scale = keep.tile([P, 1], F32)
         nc.vector.tensor_scalar(
             out=neg_scale[:], in0=scale_bf16[:], scalar1=-1.0, scalar2=None, op0=ALU.mult
         )
-        score("q")
+        score("k", whole)
+        add_bias("q", halves)
+        score("q", halves)
 
         neg_z = {}
         neg_max = {}

@@ -25,6 +25,12 @@ WARM_PASSES = 6
 FLOPS = 2 * (2 * S * D * E) + 2 * (2 * S * E * NS)
 
 
+def transpose_halves(nc, bank_cols, rows_bf16, ident):
+    words = rows_bf16.bitcast(F32).rearrange("r (u p) -> r u p", u=HALVES)
+    for u in range(HALVES):
+        nc.tensor.transpose(bank_cols[:, u, :], words[:, u, :], ident)
+
+
 def transpose_every_second_word(nc, bank_cols, rows_bf16, ident):
     words = rows_bf16.bitcast(F32).rearrange("r (p u) -> r u p", u=HALVES)
     for u in range(HALVES):
@@ -52,7 +58,15 @@ def tile_slotmemoryphasor_pa_s_kernel(
             cols = slice(g * K_PASS, (g + 1) * K_PASS)
             nc.sync.dma_start(out=x_rows[:, cols], in_=x_flat[:, cols])
         w_rows = {}
+        bias_rows = keep.tile([P, 2 * P], BF16)
+        nc.vector.memset(bias_rows[:].bitcast(F32), 0.0)
         for name, g in chunks:
+            if (name, g) == chunks[1]:
+                for row, vector in ((0, "k"), (HALVES, "q")):
+                    nc.sync.dma_start(
+                        out=bias_rows[row : row + HALVES, :],
+                        in_=biases[vector].rearrange("(u w) -> u w", u=HALVES),
+                    )
             w_rows[name, g] = keep.tile([P, PACK, E], BF16, name="w_rows_%s%d" % (name, g))
             nc.sync.dma_start(
                 out=w_rows[name, g][:],
@@ -66,13 +80,7 @@ def tile_slotmemoryphasor_pa_s_kernel(
         )
 
         scale_bf16 = keep.tile([P, 1], BF16)
-        bias = {}
         with nc.allow_non_contiguous_dma(reason="a few bytes for each partition"):
-            for name in ("k", "q"):
-                bias[name] = keep.tile([P, E_TILES], BF16, name="bias_%s" % name)
-                nc.sync.dma_start(
-                    out=bias[name][:], in_=biases[name].rearrange("(m t) -> m t", t=E_TILES)
-                )
             nc.sync.dma_start(out=scale_bf16[:], in_=scale.partition_broadcast(P))
 
         warm = keep.tile([P, 1], F32)
@@ -106,8 +114,6 @@ def tile_slotmemoryphasor_pa_s_kernel(
         for name in ("k", "q"):
             w_codes[name] = keep.tile([P, D_PASSES, E], U32, name="w_codes_%s" % name, align_bytes=64)
             w_scales[name] = keep.tile([P, D_PASSES, E], U8, name="w_scales_%s" % name, align_bytes=64)
-        by_vector = slice(0, E_TILES // 2)
-        by_scalar = slice(E_TILES // 2, E_TILES)
         half = E // 2
         one_step_late = [
             (
@@ -120,10 +126,10 @@ def tile_slotmemoryphasor_pa_s_kernel(
             w_grouped = keep.tile(
                 [P, E_TILES, P, PACK], BF16, name="w_grouped_%s%d" % (name, g), align_bytes=64
             )
-            source = w_rows[name, g][:].rearrange("p j (m t) -> p m j t", t=E_TILES)
-            target = w_grouped[:].rearrange("p t m j -> p m j t")
-            nc.vector.tensor_copy(out=target[:, :, :, by_vector], in_=source[:, :, :, by_vector])
-            nc.scalar.copy(out=target[:, :, :, by_scalar], in_=source[:, :, :, by_scalar])
+            source = w_rows[name, g][:].rearrange("p j (u m i) -> p u m j i", u=HALVES, i=2)
+            target = w_grouped[:].rearrange("p (u i) m j -> p u m j i", u=HALVES)
+            nc.vector.tensor_copy(out=target[:, 0], in_=source[:, 0])
+            nc.scalar.copy(out=target[:, 1], in_=source[:, 1])
             flat = w_grouped[:].rearrange("p t m j -> p (t m j)")
             vector_half, scalar_half = [
                 (
@@ -156,10 +162,12 @@ def tile_slotmemoryphasor_pa_s_kernel(
                         stop=(g == D_PASSES - 1),
                     )
 
-        unread_bank = psum.tile([S, D_PASSES * S], F32)
+        unread_bank = psum.tile([P, (D_PASSES + 1) * S], F32)
+        bias_bank = unread_bank[:, D_PASSES * S :]
+        nc.tensor.transpose(bias_bank, bias_rows[:].bitcast(F32), ident[:])
         for repeat in range(WARM_PASSES):
             nc.tensor.matmul_mx(
-                out=unread_bank[:],
+                out=unread_bank[:, 0 : D_PASSES * S],
                 lhsT=x_codes[:, 0, :].bitcast(FP8X4),
                 lhsT_scale=x_scales[:, 0, :],
                 rhs=x_codes[:].rearrange("p g s -> p (g s)").bitcast(FP8X4),
@@ -170,9 +178,16 @@ def tile_slotmemoryphasor_pa_s_kernel(
 
         project("k")
 
+        bias_words = keep.tile([P, 2 * HALVES], F32)
+        nc.scalar.copy(out=bias_words[:], in_=bias_bank[:, 0 : 2 * HALVES])
+        bias = {
+            name: bias_words[:].bitcast(BF16)[:, c : c + E_TILES]
+            for name, c in (("k", 0), ("q", E_TILES))
+        }
+
         slot_bank = psum.tile([P, HALVES, NS], F32)
         for h in range(SLOT_TILES):
-            transpose_every_second_word(
+            transpose_halves(
                 nc, slot_bank[:, :, h * P : (h + 1) * P], slot_rows[:, h, :], ident[:]
             )
         slot_grouped = keep.tile([P, NS * PACK], BF16, align_bytes=64)
@@ -196,7 +211,7 @@ def tile_slotmemoryphasor_pa_s_kernel(
                 nc.vector.tensor_tensor(
                     out=key_grouped[name][:, tokens, :],
                     in0=proj[name][:, :, tokens].rearrange("m t s -> m s t"),
-                    in1=bias[name][:].unsqueeze(1).to_broadcast([P, count, E_TILES]),
+                    in1=bias[name].unsqueeze(1).to_broadcast([P, count, E_TILES]),
                     op=ALU.add,
                 )
 

@@ -20,6 +20,7 @@ S, D, E, NS = 128, 1024, 512, 256
 D_PASSES = D // K_PASS
 E_TILES = E // P
 SLOT_TILES = NS // P
+VECTOR_PART = 16
 WARM_PASSES = 6
 
 FLOPS = 2 * (2 * S * D * E) + 2 * (2 * S * E * NS)
@@ -129,7 +130,10 @@ def tile_slotmemoryphasor_pa_s_kernel(
             source = w_rows[name, g][:].rearrange("p j (u m i) -> p u m j i", u=HALVES, i=2)
             target = w_grouped[:].rearrange("p (u i) m j -> p u m j i", u=HALVES)
             nc.vector.tensor_copy(out=target[:, 0], in_=source[:, 0])
-            nc.scalar.copy(out=target[:, 1], in_=source[:, 1])
+            part = VECTOR_PART if (name, g) == chunks[-1] else 0
+            if part:
+                nc.vector.tensor_copy(out=target[:, 1, :part], in_=source[:, 1, :part])
+            nc.scalar.copy(out=target[:, 1, part:], in_=source[:, 1, part:])
             flat = w_grouped[:].rearrange("p t m j -> p (t m j)")
             vector_half, scalar_half = [
                 (
@@ -143,8 +147,7 @@ def tile_slotmemoryphasor_pa_s_kernel(
                 quantise(*job)
             quantise(*vector_half)
             one_step_late = [scalar_half]
-        for job in one_step_late:
-            quantise(*job)
+        (last_half,) = one_step_late
 
         proj = {}
 
@@ -195,59 +198,66 @@ def tile_slotmemoryphasor_pa_s_kernel(
             out=slot_grouped[:].bitcast(F32).rearrange("p (n u) -> p n u", u=HALVES),
             in_=slot_bank[:].rearrange("p u n -> p n u"),
         )
+        neg_scale = keep.tile([P, 1], F32)
+        nc.scalar.mul(neg_scale[:], scale_bf16[:], -1.0)
         slot_codes = keep.tile([P, NS], U32, align_bytes=64)
         slot_scales = keep.tile([P, NS], U8, align_bytes=64)
 
-        project("q")
 
         key_grouped = {}
-
-        def add_bias(name, parts):
+        key_codes = {}
+        key_scales = {}
+        scores = {}
+        for name in ("k", "q"):
             key_grouped[name] = keep.tile(
                 [P, S, PACK], BF16, name="key_grouped_%s" % name, align_bytes=64
             )
-            for tokens in parts:
-                count = tokens.stop - tokens.start
-                nc.vector.tensor_tensor(
-                    out=key_grouped[name][:, tokens, :],
-                    in0=proj[name][:, :, tokens].rearrange("m t s -> m s t"),
-                    in1=bias[name].unsqueeze(1).to_broadcast([P, count, E_TILES]),
-                    op=ALU.add,
-                )
-
-        scores = {}
-
-        def score(name, parts):
-            key_codes = keep.tile([P, S], U32, name="key_codes_%s" % name, align_bytes=64)
-            key_scales = keep.tile([P, S], U8, name="key_scales_%s" % name, align_bytes=64)
-            for tokens in parts:
-                quantise(
-                    key_codes[:, tokens],
-                    key_scales[:, tokens],
-                    key_grouped[name][:, tokens, :].rearrange("m s t -> m (s t)"),
-                )
+            key_codes[name] = keep.tile([P, S], U32, name="key_codes_%s" % name, align_bytes=64)
+            key_scales[name] = keep.tile([P, S], U8, name="key_scales_%s" % name, align_bytes=64)
             scores[name] = psum.tile([S, NS], F32, name="scores_%s" % name)
+
+        def add_bias(name, tokens):
+            count = tokens.stop - tokens.start
+            nc.vector.tensor_tensor(
+                out=key_grouped[name][:, tokens, :],
+                in0=proj[name][:, :, tokens].rearrange("m t s -> m s t"),
+                in1=bias[name].unsqueeze(1).to_broadcast([P, count, E_TILES]),
+                op=ALU.add,
+            )
+
+        def quantise_key(name, tokens):
+            quantise(
+                key_codes[name][:, tokens],
+                key_scales[name][:, tokens],
+                key_grouped[name][:, tokens, :].rearrange("m s t -> m (s t)"),
+            )
+
+        def score(name):
             nc.tensor.matmul_mx(
                 out=scores[name][:],
-                lhsT=key_codes[:].bitcast(FP8X4),
-                lhsT_scale=key_scales[:],
+                lhsT=key_codes[name][:].bitcast(FP8X4),
+                lhsT_scale=key_scales[name][:],
                 rhs=slot_codes[:].bitcast(FP8X4),
                 rhs_scale=slot_scales[:],
                 start=True,
                 stop=True,
             )
 
-        whole = [slice(0, S)]
-        halves = [slice(0, S // 2), slice(S // 2, S)]
-        add_bias("k", whole)
+        every = slice(0, S)
+        early, late = slice(0, S // 2), slice(S // 2, S)
+        for tile in range(2):
+            part = slice(tile * P, (tile + 1) * P)
+            quantise(last_half[0][:, part], last_half[1][:, part], last_half[2][:, tile * P * PACK : (tile + 1) * P * PACK])
+        project("q")
+        add_bias("k", every)
         quantise(slot_codes[:], slot_scales[:], slot_grouped[:])
-        neg_scale = keep.tile([P, 1], F32)
-        nc.vector.tensor_scalar(
-            out=neg_scale[:], in0=scale_bf16[:], scalar1=-1.0, scalar2=None, op0=ALU.mult
-        )
-        score("k", whole)
-        add_bias("q", halves)
-        score("q", halves)
+        quantise_key("k", every)
+        score("k")
+        add_bias("q", early)
+        add_bias("q", late)
+        quantise_key("q", early)
+        quantise_key("q", late)
+        score("q")
 
         neg_z = {}
         neg_max = {}

@@ -168,16 +168,20 @@ def tile_slotmemoryphasor_pa_s_kernel(
         unread_bank = psum.tile([P, (D_PASSES + 1) * S], F32)
         bias_bank = unread_bank[:, D_PASSES * S :]
         nc.tensor.transpose(bias_bank, bias_rows[:].bitcast(F32), ident[:])
-        for repeat in range(WARM_PASSES):
-            nc.tensor.matmul_mx(
-                out=unread_bank[:, 0 : D_PASSES * S],
-                lhsT=x_codes[:, 0, :].bitcast(FP8X4),
-                lhsT_scale=x_scales[:, 0, :],
-                rhs=x_codes[:].rearrange("p g s -> p (g s)").bitcast(FP8X4),
-                rhs_scale=x_scales[:].rearrange("p g s -> p (g s)"),
-                start=True,
-                stop=True,
-            )
+
+        def keep_busy(passes):
+            for repeat in range(passes):
+                nc.tensor.matmul_mx(
+                    out=unread_bank[:, 0 : D_PASSES * S],
+                    lhsT=x_codes[:, 0, :].bitcast(FP8X4),
+                    lhsT_scale=x_scales[:, 0, :],
+                    rhs=x_codes[:].rearrange("p g s -> p (g s)").bitcast(FP8X4),
+                    rhs_scale=x_scales[:].rearrange("p g s -> p (g s)"),
+                    start=True,
+                    stop=True,
+                )
+
+        keep_busy(WARM_PASSES)
 
         project("k")
 
@@ -249,6 +253,7 @@ def tile_slotmemoryphasor_pa_s_kernel(
             part = slice(tile * P, (tile + 1) * P)
             quantise(last_half[0][:, part], last_half[1][:, part], last_half[2][:, tile * P * PACK : (tile + 1) * P * PACK])
         project("q")
+        keep_busy(2)
         add_bias("k", every)
         quantise(slot_codes[:], slot_scales[:], slot_grouped[:])
         quantise_key("k", every)

from contextlib import ExitStack

import concourse.mybir as mybir
from concourse.masks import make_identity

BF16 = mybir.dt.bfloat16
F32 = mybir.dt.float32
U32 = mybir.dt.uint32
U8 = mybir.dt.uint8
FP8X4 = mybir.dt.float8_e4m3fn_x4
ALU = mybir.AluOpType
ACT = mybir.ActivationFunctionType

P = 128
PACK = 4
K_PASS = P * PACK
HALVES = 2

S, D, E, NS = 128, 1024, 512, 256
D_PASSES = D // K_PASS
E_TILES = E // P
SLOT_TILES = NS // P
VECTOR_PART = 16
WARM_PASSES = 6

FLOPS = 2 * (2 * S * D * E) + 2 * (2 * S * E * NS)


def transpose_halves(nc, bank_cols, rows_bf16, ident):
    words = rows_bf16.bitcast(F32).rearrange("r (u p) -> r u p", u=HALVES)
    for u in range(HALVES):
        nc.tensor.transpose(bank_cols[:, u, :], words[:, u, :], ident)


def transpose_every_second_word(nc, bank_cols, rows_bf16, ident):
    words = rows_bf16.bitcast(F32).rearrange("r (p u) -> r u p", u=HALVES)
    for u in range(HALVES):
        nc.tensor.transpose(bank_cols[:, u, :], words[:, u, :], ident)


def tile_slotmemoryphasor_pa_s_kernel(
    tc, x, Wk, bk, Wq, bq, slot_keys, scale, out_0, out_1
):
    nc = tc.nc
    weights = {"k": Wk, "q": Wq}
    biases = {"k": bk, "q": bq}
    outputs = {"k": out_0, "q": out_1}

    chunks = [(name, g) for name in ("k", "q") for g in range(D_PASSES)]

    with ExitStack() as ctx:
        keep = ctx.enter_context(tc.tile_pool(name="keep", bufs=1))
        psum = ctx.enter_context(tc.psum_pool(name="psum", bufs=1))
        ctx.enter_context(tc.manual_schedule())

        x_rows = keep.tile([S, D], BF16)
        x_flat = x.flatten_outer_dims()
        for g in range(D_PASSES):
            cols = slice(g * K_PASS, (g + 1) * K_PASS)
            nc.sync.dma_start(out=x_rows[:, cols], in_=x_flat[:, cols])
        w_rows = {}
        bias_rows = keep.tile([P, 2 * P], BF16)
        nc.vector.memset(bias_rows[:].bitcast(F32), 0.0)
        for name, g in chunks:
            if (name, g) == chunks[1]:
                for row, vector in ((0, "k"), (HALVES, "q")):
                    nc.sync.dma_start(
                        out=bias_rows[row : row + HALVES, :],
                        in_=biases[vector].rearrange("(u w) -> u w", u=HALVES),
                    )
            w_rows[name, g] = keep.tile([P, PACK, E], BF16, name="w_rows_%s%d" % (name, g))
            nc.sync.dma_start(
                out=w_rows[name, g][:],
                in_=weights[name][g * K_PASS : (g + 1) * K_PASS, :].rearrange(
                    "(p j) e -> p j e", j=PACK
                ),
            )
        slot_rows = keep.tile([P, SLOT_TILES, E], BF16)
        nc.sync.dma_start(
            out=slot_rows[:], in_=slot_keys.rearrange("(h n) e -> n h e", n=P)
        )

        scale_bf16 = keep.tile([P, 1], BF16)
        with nc.allow_non_contiguous_dma(reason="a few bytes for each partition"):
            nc.sync.dma_start(out=scale_bf16[:], in_=scale.partition_broadcast(P))

        warm = keep.tile([P, 1], F32)
        nc.vector.memset(warm[:], 0.0)
        nc.scalar.activation(out=warm[:], in_=warm[:], func=ACT.Exp)

        ident = keep.tile([P, P], F32)
        make_identity(nc, ident[:])

        def quantise(codes, scales, grouped):
            nc.vector.quantize_mx(out=codes.bitcast(FP8X4), scales=scales, in_=grouped)

        x_banks = []
        for g in range(D_PASSES):
            x_bank = psum.tile([P, HALVES, S], F32, name="x_bank_%d" % g)
            transpose_every_second_word(
                nc, x_bank[:], x_rows[:, g * K_PASS : (g + 1) * K_PASS], ident[:]
            )
            x_banks.append(x_bank)
        x_grouped = keep.tile([P, D_PASSES, S * PACK], BF16, align_bytes=64)
        x_codes = keep.tile([P, D_PASSES, S], U32, align_bytes=64)
        x_scales = keep.tile([P, D_PASSES, S], U8, align_bytes=64)
        for g in range(D_PASSES):
            nc.vector.tensor_copy(
                out=x_grouped[:, g, :].bitcast(F32).rearrange("p (s u) -> p s u", u=HALVES),
                in_=x_banks[g][:].rearrange("p u s -> p s u"),
            )

        w_codes = {}
        w_scales = {}
        for name in ("k", "q"):
            w_codes[name] = keep.tile([P, D_PASSES, E], U32, name="w_codes_%s" % name, align_bytes=64)
            w_scales[name] = keep.tile([P, D_PASSES, E], U8, name="w_scales_%s" % name, align_bytes=64)
        half = E // 2
        one_step_late = [
            (
                x_codes[:].rearrange("p g s -> p (g s)"),
                x_scales[:].rearrange("p g s -> p (g s)"),
                x_grouped[:].rearrange("p g c -> p (g c)"),
            )
        ]
        for name, g in chunks:
            w_grouped = keep.tile(
                [P, E_TILES, P, PACK], BF16, name="w_grouped_%s%d" % (name, g), align_bytes=64
            )
            source = w_rows[name, g][:].rearrange("p j (u m i) -> p u m j i", u=HALVES, i=2)
            target = w_grouped[:].rearrange("p (u i) m j -> p u m j i", u=HALVES)
            nc.vector.tensor_copy(out=target[:, 0], in_=source[:, 0])
            part = VECTOR_PART if (name, g) == chunks[-1] else 0
            if part:
                nc.vector.tensor_copy(out=target[:, 1, :part], in_=source[:, 1, :part])
            nc.scalar.copy(out=target[:, 1, part:], in_=source[:, 1, part:])
            flat = w_grouped[:].rearrange("p t m j -> p (t m j)")
            vector_half, scalar_half = [
                (
                    w_codes[name][:, g, c : c + half],
                    w_scales[name][:, g, c : c + half],
                    flat[:, c * PACK : (c + half) * PACK],
                )
                for c in range(0, E, half)
            ]
            for job in one_step_late:
                quantise(*job)
            quantise(*vector_half)
            one_step_late = [scalar_half]
        (last_half,) = one_step_late

        proj = {}

        def project(name):
            proj[name] = psum.tile([P, E_TILES, S], F32, name="proj_%s" % name)
            for t in range(E_TILES):
                for g in range(D_PASSES):
                    nc.tensor.matmul_mx(
                        out=proj[name][:, t, :],
                        lhsT=w_codes[name][:, g, t * P : (t + 1) * P].bitcast(FP8X4),
                        lhsT_scale=w_scales[name][:, g, t * P : (t + 1) * P],
                        rhs=x_codes[:, g, :].bitcast(FP8X4),
                        rhs_scale=x_scales[:, g, :],
                        start=(g == 0),
                        stop=(g == D_PASSES - 1),
                    )

        unread_bank = psum.tile([P, (D_PASSES + 1) * S], F32)
        bias_bank = unread_bank[:, D_PASSES * S :]
        nc.tensor.transpose(bias_bank, bias_rows[:].bitcast(F32), ident[:])

        def keep_busy(passes):
            for repeat in range(passes):
                nc.tensor.matmul_mx(
                    out=unread_bank[:, 0 : D_PASSES * S],
                    lhsT=x_codes[:, 0, :].bitcast(FP8X4),
                    lhsT_scale=x_scales[:, 0, :],
                    rhs=x_codes[:].rearrange("p g s -> p (g s)").bitcast(FP8X4),
                    rhs_scale=x_scales[:].rearrange("p g s -> p (g s)"),
                    start=True,
                    stop=True,
                )

        keep_busy(WARM_PASSES)

        project("k")

        bias_words = keep.tile([P, 2 * HALVES], F32)
        nc.scalar.copy(out=bias_words[:], in_=bias_bank[:, 0 : 2 * HALVES])
        bias = {
            name: bias_words[:].bitcast(BF16)[:, c : c + E_TILES]
            for name, c in (("k", 0), ("q", E_TILES))
        }

        slot_bank = psum.tile([P, HALVES, NS], F32)
        for h in range(SLOT_TILES):
            transpose_halves(
                nc, slot_bank[:, :, h * P : (h + 1) * P], slot_rows[:, h, :], ident[:]
            )
        slot_grouped = keep.tile([P, NS * PACK], BF16, align_bytes=64)
        nc.scalar.copy(
            out=slot_grouped[:].bitcast(F32).rearrange("p (n u) -> p n u", u=HALVES),
            in_=slot_bank[:].rearrange("p u n -> p n u"),
        )
        neg_scale = keep.tile([P, 1], F32)
        nc.scalar.mul(neg_scale[:], scale_bf16[:], -1.0)
        slot_codes = keep.tile([P, NS], U32, align_bytes=64)
        slot_scales = keep.tile([P, NS], U8, align_bytes=64)


        key_grouped = {}
        key_codes = {}
        key_scales = {}
        scores = {}
        for name in ("k", "q"):
            key_grouped[name] = keep.tile(
                [P, S, PACK], BF16, name="key_grouped_%s" % name, align_bytes=64
            )
            key_codes[name] = keep.tile([P, S], U32, name="key_codes_%s" % name, align_bytes=64)
            key_scales[name] = keep.tile([P, S], U8, name="key_scales_%s" % name, align_bytes=64)
            scores[name] = psum.tile([S, NS], F32, name="scores_%s" % name)

        def add_bias(name, tokens):
            count = tokens.stop - tokens.start
            nc.vector.tensor_tensor(
                out=key_grouped[name][:, tokens, :],
                in0=proj[name][:, :, tokens].rearrange("m t s -> m s t"),
                in1=bias[name].unsqueeze(1).to_broadcast([P, count, E_TILES]),
                op=ALU.add,
            )

        def quantise_key(name, tokens):
            quantise(
                key_codes[name][:, tokens],
                key_scales[name][:, tokens],
                key_grouped[name][:, tokens, :].rearrange("m s t -> m (s t)"),
            )

        def score(name):
            nc.tensor.matmul_mx(
                out=scores[name][:],
                lhsT=key_codes[name][:].bitcast(FP8X4),
                lhsT_scale=key_scales[name][:],
                rhs=slot_codes[:].bitcast(FP8X4),
                rhs_scale=slot_scales[:],
                start=True,
                stop=True,
            )

        every = slice(0, S)
        early, late = slice(0, S // 2), slice(S // 2, S)
        for tile in range(2):
            part = slice(tile * P, (tile + 1) * P)
            quantise(last_half[0][:, part], last_half[1][:, part], last_half[2][:, tile * P * PACK : (tile + 1) * P * PACK])
        project("q")
        keep_busy(2)
        add_bias("k", every)
        quantise(slot_codes[:], slot_scales[:], slot_grouped[:])
        quantise_key("k", every)
        score("k")
        add_bias("q", early)
        add_bias("q", late)
        quantise_key("q", early)
        quantise_key("q", late)
        score("q")

        neg_z = {}
        neg_max = {}
        for name in ("k", "q"):
            neg_z[name] = keep.tile([S, NS], F32, name="neg_z_%s" % name)
            neg_max[name] = keep.tile([S, 1], F32, name="neg_max_%s" % name)
            nc.vector.tensor_scalar(
                out=neg_z[name][:],
                in0=scores[name][:],
                scalar1=neg_scale[:, 0:1],
                scalar2=None,
                op0=ALU.mult,
                op1=ALU.min,
                accum_out=neg_max[name][:],
            )
        for name in ("k", "q"):
            exp_z = keep.tile([S, NS], F32, name="exp_z_%s" % name)
            total = keep.tile([S, 1], F32, name="total_%s" % name)
            nc.scalar.activation(
                out=exp_z[:],
                in_=neg_z[name][:],
                func=ACT.Exp,
                bias=neg_max[name][:, 0:1],
                scale=-1.0,
                accum_out=total[:],
            )
            inverse = keep.tile([S, 1], F32, name="inverse_%s" % name)
            nc.vector.reciprocal(out=inverse[:], in_=total[:])
            weights_out = keep.tile([S, NS], F32, name="weights_out_%s" % name)
            nc.vector.tensor_scalar(
                out=weights_out[:], in0=exp_z[:], scalar1=inverse[:, 0:1], scalar2=None, op0=ALU.mult
            )
            nc.sync.dma_start(out=outputs[name].flatten_outer_dims(), in_=weights_out[:])
